import numpy as np
import ml_dtypes


def mxq(x, axis, fmt="e4m3"):
    dtype, down = {"e4m3": (ml_dtypes.float8_e4m3fn, 7), "e5m2": (ml_dtypes.float8_e5m2, 14)}[fmt]
    v = np.moveaxis(np.asarray(x, np.float32).astype(ml_dtypes.bfloat16).astype(np.float64), axis, -1)
    blocks = v.reshape(v.shape[:-1] + (-1, 32))
    amax = np.abs(blocks).max(-1, keepdims=True)
    byte = np.maximum(np.where(amax > 0, np.frexp(amax)[1] - 1 + 127, 0) - down, 1)
    scale = np.exp2(byte - 127.0)
    codes = (blocks / scale).astype(np.float32).astype(dtype).astype(np.float64)
    return np.moveaxis((codes * scale).reshape(v.shape), -1, axis)


WIDE = False


def mx_kscale(k):
    if not WIDE:
        return np.ones(k)
    levels = np.array([10, -10, 5, -5, 0])
    if k % 512:
        return np.exp2(np.random.permutation(np.resize(levels, k // 32))).repeat(32)
    a = np.empty((k // 512, 16))
    for p in range(k // 512):
        a[p, :8] = np.random.permutation(np.resize(levels, 8))
        for g in range(8):
            far = levels[np.abs(levels - a[p, g]) >= 10]
            a[p, g + 8] = far[np.random.randint(len(far))]
    return np.exp2(a.ravel()).repeat(32)


BF16 = ml_dtypes.bfloat16


def bf(x):
    return np.asarray(x, np.float32).astype(BF16)


def f64(x):
    return np.asarray(x).astype(np.float64)


S, B, SC = 4096, 1024, 1024


def setup_inputs():
    s = mx_kscale(B)
    return {"proba": bf((np.random.standard_normal((S, B)) * s).reshape(-1)),
            "cur_inven": bf(np.random.random_sample((S, SC))),
            "bun_sc": bf(np.random.random_sample((B, SC)) * (16.0 / np.sqrt(B)) / s[:, None]),
            "avail_bundle": bf(np.random.random_sample(B) * s),
            "alloc_bundle": bf(np.random.random_sample(B) * s)}


def reference(proba, cur_inven, bun_sc, avail_bundle, alloc_bundle):
    p = f64(proba).reshape(S, B)
    av = f64(avail_bundle)
    al = f64(alloc_bundle)
    over_avail = (av[None, :] - p < 0.0) & (p > 0.0)
    over_alloc = (al[None, :] + p < 0.0) & (p < 0.0)
    cm = np.where(over_avail | over_alloc, 0.01, 1.0)
    next_inven = f64(cur_inven) + (mxq(p * cm, 1, "e4m3") @ mxq(f64(bun_sc), 0, "e4m3"))
    return next_inven.reshape(1, -1)

@@ -1,0 +1,284 @@
+from contextlib import ExitStack
+
+import concourse.mybir as mybir
+from concourse.masks import make_identity
+
+FP8X4 = mybir.dt.float8_e4m3fn_x4
+BF16 = mybir.dt.bfloat16
+F32 = mybir.dt.float32
+U32 = mybir.dt.uint32
+U8 = mybir.dt.uint8
+ALU = mybir.AluOpType
+
+S, B, SC = 4096, 1024, 1024
+FLOPS = 2 * S * B * SC
+
+P = 128
+JT = 4
+ROWS = P * JT
+NST = S // ROWS
+G = B // 512
+NU = NST * G
+PIN = True
+VEC_EVERY = 1
+
+
+def tile_optblockv2_t_kernel(tc, proba, cur_inven, bun_sc, avail_bundle, alloc_bundle, out):
+    nc = tc.nc
+    xv = proba.rearrange("(i r j k) -> i r j k", r=P, j=JT, k=B)
+    cv = cur_inven.rearrange("(i r j) n -> i r (j n)", r=P, j=JT)
+    ov = out.rearrange("o (i r q) -> (o i) r q", r=P, q=JT * SC)
+    bv = bun_sc.rearrange("(g p t) n -> g p t n", t=4, p=P)
+
+    units = []
+    for i in range(NST - 1):
+        for g in range(G):
+            units.append([(i, g, 0), (i, g, 1)])
+    for b in range(2):
+        units.append([(NST - 1, 0, b), (NST - 1, 1, b)])
+
+    with ExitStack() as ctx:
+        const = ctx.enter_context(tc.tile_pool(name="const", bufs=1))
+        xin = ctx.enter_context(tc.tile_pool(name="xin", bufs=3))
+        cin = ctx.enter_context(tc.tile_pool(name="cin", bufs=4))
+        oout = ctx.enter_context(tc.tile_pool(name="oout", bufs=3))
+        work = ctx.enter_context(tc.tile_pool(name="work", bufs=2))
+        xtp = ctx.enter_context(tc.psum_pool(name="xtp", bufs=4))
+        accp = ctx.enter_context(tc.psum_pool(name="accp", bufs=4))
+        if PIN:
+            ctx.enter_context(tc.manual_schedule())
+
+        x_t = {}
+        c_t = {}
+        o_t = {}
+        banks = {}
+        xs_t = {}
+        cl_t = {}
+        h_t = {}
+        words = {}
+        bgrp = {}
+
+        ident = const.tile([P, P], BF16)
+        make_identity(nc, ident[:])
+        vt_av = const.tile([P, G, 4], BF16)
+        vt_al = const.tile([P, G, 4], BF16)
+        braw = const.tile([P, 2 * 4, SC], BF16)
+        bcodes = const.tile([P, G, SC], U32, align_bytes=64)
+        bscl = const.tile([P, G, SC], U8, align_bytes=64)
+        thr = const.tile([P, 16], F32)
+
+        def load_b(g):
+            nc.sync.dma_start(out=braw[:, 4 * g : 4 * g + 4, :], in_=bv[g])
+
+        def load_x(i, by_pass=False):
+            xt = xin.tile([P, JT, B], BF16, name="xt")
+            if by_pass:
+                nc.sync.dma_start(out=xt[:, 0:2, 0:512], in_=xv[i][:, 0:2, 0:512])
+                nc.sync.dma_start(out=xt[:, 2:4, 0:512], in_=xv[i][:, 2:4, 0:512])
+                nc.sync.dma_start(out=xt[:, :, 512:1024], in_=xv[i][:, :, 512:1024])
+            else:
+                nc.sync.dma_start(out=xt[:], in_=xv[i])
+            x_t[i] = xt
+
+        def load_c(i):
+            ct = cin.tile([P, JT, SC], BF16, name="ct")
+            nc.sync.dma_start(out=ct[:].rearrange("p j n -> p (j n)"), in_=cv[i])
+            c_t[i] = ct
+
+        def regroup_b(g, eng):
+            bg = const.tile([P, SC, 4], BF16, align_bytes=64, name="bgrp%d" % g)
+            dst = bg[:].rearrange("p (c i) t -> p c t i", i=4)
+            src = braw[:, 4 * g : 4 * g + 4, :].rearrange("p t (c i) -> p c t i", i=4)
+            if eng == "v":
+                nc.vector.tensor_copy(out=dst, in_=src)
+            elif eng == "s":
+                nc.scalar.copy(out=dst, in_=src)
+            else:
+                nc.gpsimd.tensor_scalar(out=dst, in0=src, scalar1=1.0, scalar2=0.0, op0=ALU.mult, op1=ALU.add)
+            bgrp[g] = bg
+
+        def quant_b(g):
+            nc.vector.quantize_mx(
+                out=bcodes[:, g, :].bitcast(FP8X4),
+                scales=bscl[:, g, :],
+                in_=bgrp[g][:].rearrange("p n t -> p (n t)"),
+            )
+
+        def transposes(v):
+            for a, (i, g, b) in enumerate(units[v]):
+                bank = xtp.tile([P, 4, 256], BF16, tag="xt", name="bank")
+                for t in range(4):
+                    for jj in range(2):
+                        k0 = 512 * g + t
+                        nc.tensor.transpose(
+                            bank[:, t, 128 * jj : 128 * jj + 128], x_t[i][:, 2 * b + jj, k0 : 512 * (g + 1) : 4], ident[:]
+                        )
+                banks[(v, a)] = bank
+
+        def copies(v):
+            xs = work.tile([P, 2, 4, 256], BF16, name="xs", bufs=3)
+            for a in range(2):
+                nc.scalar.copy(out=xs[:, a, :, :], in_=banks[(v, a)][:])
+            xs_t[v] = xs
+
+        def clamp(dst, src, ch):
+            nc.vector.tensor_scalar(
+                out=dst,
+                in0=src,
+                scalar1=thr[:, 8 + ch : 9 + ch],
+                scalar2=thr[:, ch : ch + 1],
+                op0=ALU.max,
+                op1=ALU.min,
+            )
+
+        def clamps(v):
+            cl = work.tile([P, 2, 4, 256], BF16, name="cl")
+            xs = xs_t[v]
+            g0 = units[v][0][1]
+            g1 = units[v][1][1]
+            if g0 == g1 and v > 0:
+                for t in range(4):
+                    clamp(cl[:, :, t, :], xs[:, :, t, :], 4 * g0 + t)
+            else:
+                for a, ga in enumerate((g0, g1)):
+                    for t in range(4):
+                        clamp(cl[:, a, t, :], xs[:, a, t, :], 4 * ga + t)
+            cl_t[v] = cl
+
+        def damp(v):
+            cl = cl_t[v]
+            kp = work.tile([P, 2, 4, 256], BF16, name="kp")
+            h = work.tile([P, 2, 256, 4], BF16, align_bytes=64, name="h")
+            for a in range(2):
+                nc.vector.tensor_tensor(out=kp[:, a, :, :], in0=cl[:, a, :, :], in1=banks[(v, a)][:], op=ALU.is_equal)
+            for a in range(2):
+                nc.vector.scalar_tensor_tensor(
+                    out=h[:, a, :, :],
+                    in0=kp[:, a, :, :].rearrange("p t s -> p s t"),
+                    scalar=0.01,
+                    in1=banks[(v, a)][:].rearrange("p t s -> p s t"),
+                    op0=ALU.max,
+                    op1=ALU.mult,
+                )
+            h_t[v] = h
+
+        def quant(v):
+            codes = work.tile([P, 2, 256], U32, align_bytes=64, name="codes", bufs=5)
+            scl = work.tile([P, 2, 256], U8, align_bytes=64, name="scl", bufs=5)
+            nc.vector.quantize_mx(
+                out=codes[:].rearrange("p a s -> p (a s)").bitcast(FP8X4),
+                scales=scl[:].rearrange("p a s -> p (a s)"),
+                in_=h_t[v][:].rearrange("p a s t -> p (a s t)"),
+            )
+            for a, key in enumerate(units[v]):
+                words[key] = (codes[:, a, :], scl[:, a, :])
+
+        def add_cur_vector(i, acc, j, hf):
+            cols = slice(512 * hf, 512 * hf + 512)
+            nc.vector.tensor_tensor(out=o_t[i][:, j, cols], in0=acc[:], in1=c_t[i][:, j, cols], op=ALU.add)
+
+        def job(i, b, vec_later=(), vec_now=False):
+            if b == 0:
+                ot = oout.tile([P, JT, SC], F32, name="ot")
+                o_t[i] = ot
+            later = []
+            for n in range(4):
+                jj, hf = divmod(n, 2)
+                j = 2 * b + jj
+                acc = accp.tile([P, 512], F32, name="acc")
+                for g in range(G):
+                    cw, sw = words[(i, g, b)]
+                    nc.tensor.matmul_mx(
+                        out=acc[:],
+                        lhsT=cw[:, 128 * jj : 128 * jj + 128].bitcast(FP8X4),
+                        lhsT_scale=sw[:, 128 * jj : 128 * jj + 128],
+                        rhs=bcodes[:, g, 512 * hf : 512 * hf + 512].bitcast(FP8X4),
+                        rhs_scale=bscl[:, g, 512 * hf : 512 * hf + 512],
+                        start=(g == 0),
+                        stop=(g == G - 1),
+                    )
+                cols = slice(512 * hf, 512 * hf + 512)
+                if vec_now:
+                    add_cur_vector(i, acc, j, hf)
+                    if hf == 1:
+                        nc.sync.dma_start(out=ov[i][:, SC * j : SC * j + SC], in_=o_t[i][:, j, :])
+                elif n in vec_later:
+                    later.append((i, acc, j, hf))
+                else:
+                    nc.scalar.copy(out=o_t[i][:, j, cols], in_=acc[:])
+                    nc.gpsimd.tensor_tensor(
+                        out=o_t[i][:, j, cols], in0=o_t[i][:, j, cols], in1=c_t[i][:, j, cols], op=ALU.add
+                    )
+            return later
+
+        def store(i, b):
+            w = 2 * SC
+            nc.sync.dma_start(
+                out=ov[i][:, w * b : w * b + w], in_=o_t[i][:, 2 * b : 2 * b + 2, :].rearrange("p j n -> p (j n)")
+            )
+
+        nc.sync.dma_start(out=vt_av[:], in_=avail_bundle.rearrange("(g p t) -> p g t", p=P, t=4))
+        nc.sync.dma_start(out=vt_al[:], in_=alloc_bundle.rearrange("(g p t) -> p g t", p=P, t=4))
+        load_x(0, by_pass=True)
+        load_b(0)
+        load_b(1)
+        load_x(1)
+        load_c(0)
+        load_x(2)
+        load_c(1)
+
+        nc.vector.tensor_scalar(out=thr[:, 0:8], in0=vt_av[:].rearrange("p g t -> p (g t)"), scalar1=0.0, scalar2=None, op0=ALU.max)
+        nc.vector.tensor_scalar(
+            out=thr[:, 8:16], in0=vt_al[:].rearrange("p g t -> p (g t)"), scalar1=-1.0, scalar2=0.0, op0=ALU.mult, op1=ALU.min
+        )
+        transposes(0)
+        copies(0)
+        transposes(1)
+        copies(1)
+        regroup_b(0, "s")
+        regroup_b(1, "g")
+
+        jobs_at = {}
+        for i in range(NST - 1):
+            jobs_at[2 * i + 2] = [(i, 0)]
+            jobs_at[2 * i + 3] = [(i, 1)]
+        jobs_at[NU - 1].append((NST - 1, 0))
+
+        count = 0
+        held = []
+        for v in range(NU):
+            m = v // 2
+            for i, b in jobs_at.get(v - 2, []):
+                store(i, b)
+            if v % 2 == 0:
+                if m + 2 < NST:
+                    load_c(m + 2)
+                if m + 3 < NST:
+                    load_x(m + 3)
+            clamps(v)
+            if v >= 1:
+                quant(v - 1)
+            if v == 2:
+                quant_b(0)
+                quant_b(1)
+            later = []
+            for i, b in jobs_at.get(v, []):
+                if i == NST - 1:
+                    held.extend(job(i, b, vec_later=(2, 3)))
+                else:
+                    count += 1
+                    take = count % 4 != 0
+                    later.extend(job(i, b, vec_later=(3,) if take else ()))
+            damp(v)
+            if v + 2 < NU:
+                transposes(v + 2)
+                copies(v + 2)
+            for i, acc, j, hf in later:
+                add_cur_vector(i, acc, j, hf)
+        quant(NU - 1)
+        for i, acc, j, hf in held:
+            add_cur_vector(i, acc, j, hf)
+        store(NST - 2, 0)
+        store(NST - 2, 1)
+        store(NST - 1, 0)
+        job(NST - 1, 1, vec_now=True)

@@ -104,8 +104,9 @@ def tile_optblockv2_t_kernel(tc, proba, cur_inven, bun_sc, avail_bundle, alloc_b
                 in_=bgrp[g][:].rearrange("p n t -> p (n t)"),
             )
 
-        def transposes(v):
-            for a, (i, g, b) in enumerate(units[v]):
+        def transposes(v, halves=(0, 1)):
+            for a in halves:
+                i, g, b = units[v][a]
                 bank = xtp.tile([P, 4, 256], BF16, tag="xt", name="bank")
                 for t in range(4):
                     for jj in range(2):
@@ -115,11 +116,12 @@ def tile_optblockv2_t_kernel(tc, proba, cur_inven, bun_sc, avail_bundle, alloc_b
                         )
                 banks[(v, a)] = bank
 
-        def copies(v):
-            xs = work.tile([P, 2, 4, 256], BF16, name="xs", bufs=3)
-            for a in range(2):
-                nc.scalar.copy(out=xs[:, a, :, :], in_=banks[(v, a)][:])
-            xs_t[v] = xs
+        def copies(v, halves=(0, 1)):
+            if 0 in halves:
+                xs = work.tile([P, 2, 4, 256], BF16, name="xs", bufs=3)
+                xs_t[v] = xs
+            for a in halves:
+                nc.scalar.copy(out=xs_t[v][:, a, :, :], in_=banks[(v, a)][:])
 
         def clamp(dst, src, ch):
             nc.vector.tensor_scalar(
@@ -177,12 +179,12 @@ def tile_optblockv2_t_kernel(tc, proba, cur_inven, bun_sc, avail_bundle, alloc_b
             cols = slice(512 * hf, 512 * hf + 512)
             nc.vector.tensor_tensor(out=o_t[i][:, j, cols], in0=acc[:], in1=c_t[i][:, j, cols], op=ALU.add)
 
-        def job(i, b, vec_later=(), vec_now=False):
-            if b == 0:
+        def job(i, b, vec_later=(), vec_now=False, tiles=(0, 1)):
+            if b == 0 and 0 in tiles:
                 ot = oout.tile([P, JT, SC], F32, name="ot")
                 o_t[i] = ot
             later = []
-            for n in range(4):
+            for n in range(2 * tiles[0], 2 * tiles[-1] + 2):
                 jj, hf = divmod(n, 2)
                 j = 2 * b + jj
                 acc = accp.tile([P, 512], F32, name="acc")
@@ -262,17 +264,25 @@ def tile_optblockv2_t_kernel(tc, proba, cur_inven, bun_sc, avail_bundle, alloc_b
                 quant_b(0)
                 quant_b(1)
             later = []
+            second = []
             for i, b in jobs_at.get(v, []):
                 if i == NST - 1:
                     held.extend(job(i, b, vec_later=(2, 3)))
+                elif v == NU - 1:
+                    later.extend(job(i, b, vec_later=(3,)))
                 else:
                     count += 1
-                    take = count % 4 != 0
-                    later.extend(job(i, b, vec_later=(3,) if take else ()))
+                    later.extend(job(i, b, vec_later=(1,) if count % 4 != 0 else (), tiles=(0,)))
+                    second.append((i, b))
             damp(v)
             if v + 2 < NU:
-                transposes(v + 2)
-                copies(v + 2)
+                transposes(v + 2, (0,))
+                copies(v + 2, (0,))
+            for i, b in second:
+                job(i, b, tiles=(1,))
+            if v + 2 < NU:
+                transposes(v + 2, (1,))
+                copies(v + 2, (1,))
             for i, acc, j, hf in later:
                 add_cur_vector(i, acc, j, hf)
         quant(NU - 1)

@@ -57,6 +57,7 @@ def tile_optblockv2_t_kernel(tc, proba, cur_inven, bun_sc, avail_bundle, alloc_b
         h_t = {}
         words = {}
         bgrp = {}
+        pend = []
 
         ident = const.tile([P, P], BF16)
         make_identity(nc, ident[:])
@@ -70,32 +71,42 @@ def tile_optblockv2_t_kernel(tc, proba, cur_inven, bun_sc, avail_bundle, alloc_b
         def load_b(g):
             nc.sync.dma_start(out=braw[:, 4 * g : 4 * g + 4, :], in_=bv[g])
 
-        def load_x(i, by_pass=False):
+        def load_x(i):
             xt = xin.tile([P, JT, B], BF16, name="xt")
-            if by_pass:
-                nc.sync.dma_start(out=xt[:, 0:2, 0:512], in_=xv[i][:, 0:2, 0:512])
-                nc.sync.dma_start(out=xt[:, 2:4, 0:512], in_=xv[i][:, 2:4, 0:512])
-                nc.sync.dma_start(out=xt[:, :, 512:1024], in_=xv[i][:, :, 512:1024])
-            else:
-                nc.sync.dma_start(out=xt[:], in_=xv[i])
+            nc.sync.dma_start(out=xt[:], in_=xv[i])
             x_t[i] = xt
+
+        x0_t = {}
+
+        def load_x0(g, b):
+            js = slice(2 * b, 2 * b + 2) if g == 0 else slice(0, JT)
+            xt = const.tile([P, js.stop - js.start, 512], BF16, name="x0_%d%d" % (g, b))
+            nc.sync.dma_start(out=xt[:], in_=xv[0][:, js, 512 * g : 512 * g + 512])
+            for j in range(js.start, js.stop):
+                x0_t[(g, j)] = xt[:, j - js.start, :]
+
+        def x_cols(i, g, j, t):
+            if i == 0:
+                return x0_t[(g, j)][:, t:512:4]
+            return x_t[i][:, j, 512 * g + t : 512 * (g + 1) : 4]
 
         def load_c(i):
             ct = cin.tile([P, JT, SC], BF16, name="ct")
             nc.sync.dma_start(out=ct[:].rearrange("p j n -> p (j n)"), in_=cv[i])
             c_t[i] = ct
 
-        def regroup_b(g, eng):
+        for g in range(G):
             bg = const.tile([P, SC, 4], BF16, align_bytes=64, name="bgrp%d" % g)
-            dst = bg[:].rearrange("p (c i) t -> p c t i", i=4)
-            src = braw[:, 4 * g : 4 * g + 4, :].rearrange("p t (c i) -> p c t i", i=4)
-            if eng == "v":
-                nc.vector.tensor_copy(out=dst, in_=src)
-            elif eng == "s":
+            bgrp[g] = bg
+
+        def regroup_b(g, half, eng):
+            cols = slice(512 * half, 512 * half + 512)
+            dst = bgrp[g][:, cols, :].rearrange("p (c i) t -> p c t i", i=4)
+            src = braw[:, 4 * g : 4 * g + 4, cols].rearrange("p t (c i) -> p c t i", i=4)
+            if eng == "s":
                 nc.scalar.copy(out=dst, in_=src)
             else:
                 nc.gpsimd.tensor_scalar(out=dst, in0=src, scalar1=1.0, scalar2=0.0, op0=ALU.mult, op1=ALU.add)
-            bgrp[g] = bg
 
         def quant_b(g):
             nc.vector.quantize_mx(
@@ -110,9 +121,8 @@ def tile_optblockv2_t_kernel(tc, proba, cur_inven, bun_sc, avail_bundle, alloc_b
                 bank = xtp.tile([P, 4, 256], BF16, tag="xt", name="bank")
                 for t in range(4):
                     for jj in range(2):
-                        k0 = 512 * g + t
                         nc.tensor.transpose(
-                            bank[:, t, 128 * jj : 128 * jj + 128], x_t[i][:, 2 * b + jj, k0 : 512 * (g + 1) : 4], ident[:]
+                            bank[:, t, 128 * jj : 128 * jj + 128], x_cols(i, g, 2 * b + jj, t), ident[:]
                         )
                 banks[(v, a)] = bank
 
@@ -179,7 +189,7 @@ def tile_optblockv2_t_kernel(tc, proba, cur_inven, bun_sc, avail_bundle, alloc_b
             cols = slice(512 * hf, 512 * hf + 512)
             nc.vector.tensor_tensor(out=o_t[i][:, j, cols], in0=acc[:], in1=c_t[i][:, j, cols], op=ALU.add)
 
-        def job(i, b, vec_later=(), vec_now=False, tiles=(0, 1)):
+        def job(i, b, vec_later=(), vec_now=False, tiles=(0, 1), wait=False):
             if b == 0 and 0 in tiles:
                 ot = oout.tile([P, JT, SC], F32, name="ot")
                 o_t[i] = ot
@@ -208,10 +218,27 @@ def tile_optblockv2_t_kernel(tc, proba, cur_inven, bun_sc, avail_bundle, alloc_b
                     later.append((i, acc, j, hf))
                 else:
                     nc.scalar.copy(out=o_t[i][:, j, cols], in_=acc[:])
-                    nc.gpsimd.tensor_tensor(
-                        out=o_t[i][:, j, cols], in0=o_t[i][:, j, cols], in1=c_t[i][:, j, cols], op=ALU.add
-                    )
+                    if hf == 0 and n + 1 not in vec_later:
+                        continue
+                    if hf == 1 and n - 1 not in vec_later:
+                        cols = slice(0, SC)
+                    if wait:
+                        pend.append((i, j, cols))
+                    else:
+                        add_cur_gpsimd(i, j, cols)
             return later
+
+        def add_cur_gpsimd(i, j, cols):
+            nc.gpsimd.tensor_tensor(
+                out=o_t[i][:, j, cols], in0=o_t[i][:, j, cols], in1=c_t[i][:, j, cols], op=ALU.add
+            )
+
+        def release(v):
+            word = work.tile([P, 1], U32, name="word")
+            nc.gpsimd.tensor_copy(out=word[:], in_=words[units[v][0]][0][:, 0:1])
+            for i, j, cols in pend:
+                add_cur_gpsimd(i, j, cols)
+            pend.clear()
 
         def store(i, b):
             w = 2 * SC
@@ -219,10 +246,12 @@ def tile_optblockv2_t_kernel(tc, proba, cur_inven, bun_sc, avail_bundle, alloc_b
                 out=ov[i][:, w * b : w * b + w], in_=o_t[i][:, 2 * b : 2 * b + 2, :].rearrange("p j n -> p (j n)")
             )
 
+        load_x0(0, 0)
         nc.sync.dma_start(out=vt_av[:], in_=avail_bundle.rearrange("(g p t) -> p g t", p=P, t=4))
         nc.sync.dma_start(out=vt_al[:], in_=alloc_bundle.rearrange("(g p t) -> p g t", p=P, t=4))
-        load_x(0, by_pass=True)
+        load_x0(0, 1)
         load_b(0)
+        load_x0(1, 0)
         load_b(1)
         load_x(1)
         load_c(0)
@@ -236,21 +265,29 @@ def tile_optblockv2_t_kernel(tc, proba, cur_inven, bun_sc, avail_bundle, alloc_b
         transposes(0)
         copies(0)
         transposes(1)
+        regroup_b(0, 0, "s")
         copies(1)
-        regroup_b(0, "s")
-        regroup_b(1, "g")
+        regroup_b(0, 1, "s")
+        regroup_b(1, 0, "s")
+        regroup_b(1, 1, "g")
 
-        jobs_at = {}
+        first = {}
+        second = {}
+        done = {}
         for i in range(NST - 1):
-            jobs_at[2 * i + 2] = [(i, 0)]
-            jobs_at[2 * i + 3] = [(i, 1)]
-        jobs_at[NU - 1].append((NST - 1, 0))
+            for b in range(2):
+                first[2 * i + b + 2] = [(i, b, 0)]
+                second[2 * i + b + 2] = [(i, b, 1)]
+                done[2 * i + b + 2] = [(i, b)]
+        second[NU - 2].append((NST - 2, 1, 0))
+        first[NU - 1] = [(NST - 2, 1, 1), (NST - 1, 0, 0)]
+        second[NU - 1] = [(NST - 1, 0, 1)]
+        done[NU - 1].append((NST - 1, 0))
 
-        count = 0
         held = []
         for v in range(NU):
             m = v // 2
-            for i, b in jobs_at.get(v - 2, []):
+            for i, b in done.get(v - 2, []):
                 store(i, b)
             if v % 2 == 0:
                 if m + 2 < NST:
@@ -260,26 +297,26 @@ def tile_optblockv2_t_kernel(tc, proba, cur_inven, bun_sc, avail_bundle, alloc_b
             clamps(v)
             if v >= 1:
                 quant(v - 1)
-            if v == 2:
-                quant_b(0)
-                quant_b(1)
+            if v in (1, 2):
+                quant_b(v - 1)
+            if pend:
+                release(v - 1)
             later = []
-            second = []
-            for i, b in jobs_at.get(v, []):
+            for i, b, tile in first.get(v, []):
                 if i == NST - 1:
-                    held.extend(job(i, b, vec_later=(2, 3)))
+                    vec = ()
                 elif v == NU - 1:
-                    later.extend(job(i, b, vec_later=(3,)))
+                    vec = (2, 3)
                 else:
-                    count += 1
-                    later.extend(job(i, b, vec_later=(1,) if count % 4 != 0 else (), tiles=(0,)))
-                    second.append((i, b))
+                    vec = (1,)
+                later.extend(job(i, b, vec_later=vec, tiles=(tile,)))
             damp(v)
             if v + 2 < NU:
                 transposes(v + 2, (0,))
                 copies(v + 2, (0,))
-            for i, b in second:
-                job(i, b, tiles=(1,))
+            for i, b, tile in second.get(v, []):
+                vec = (2, 3) if i == NST - 1 else ()
+                held.extend(job(i, b, vec_later=vec, tiles=(tile,), wait=v < NU - 2))
             if v + 2 < NU:
                 transposes(v + 2, (1,))
                 copies(v + 2, (1,))

from contextlib import ExitStack

import concourse.mybir as mybir
from concourse.masks import make_identity

FP8X4 = mybir.dt.float8_e4m3fn_x4
BF16 = mybir.dt.bfloat16
F32 = mybir.dt.float32
U32 = mybir.dt.uint32
U8 = mybir.dt.uint8
ALU = mybir.AluOpType

S, B, SC = 4096, 1024, 1024
FLOPS = 2 * S * B * SC

P = 128
JT = 4
ROWS = P * JT
NST = S // ROWS
G = B // 512
NU = NST * G
PIN = True
VEC_EVERY = 1


def tile_optblockv2_t_kernel(tc, proba, cur_inven, bun_sc, avail_bundle, alloc_bundle, out):
    nc = tc.nc
    xv = proba.rearrange("(i r j k) -> i r j k", r=P, j=JT, k=B)
    cv = cur_inven.rearrange("(i r j) n -> i r (j n)", r=P, j=JT)
    ov = out.rearrange("o (i r q) -> (o i) r q", r=P, q=JT * SC)
    bv = bun_sc.rearrange("(g p t) n -> g p t n", t=4, p=P)

    units = []
    for i in range(NST - 1):
        for g in range(G):
            units.append([(i, g, 0), (i, g, 1)])
    for b in range(2):
        units.append([(NST - 1, 0, b), (NST - 1, 1, b)])

    with ExitStack() as ctx:
        const = ctx.enter_context(tc.tile_pool(name="const", bufs=1))
        xin = ctx.enter_context(tc.tile_pool(name="xin", bufs=3))
        cin = ctx.enter_context(tc.tile_pool(name="cin", bufs=4))
        oout = ctx.enter_context(tc.tile_pool(name="oout", bufs=3))
        work = ctx.enter_context(tc.tile_pool(name="work", bufs=2))
        xtp = ctx.enter_context(tc.psum_pool(name="xtp", bufs=4))
        accp = ctx.enter_context(tc.psum_pool(name="accp", bufs=4))
        if PIN:
            ctx.enter_context(tc.manual_schedule())

        x_t = {}
        c_t = {}
        o_t = {}
        banks = {}
        xs_t = {}
        cl_t = {}
        h_t = {}
        words = {}
        bgrp = {}
        pend = []

        ident = const.tile([P, P], BF16)
        make_identity(nc, ident[:])
        vt_av = const.tile([P, G, 4], BF16)
        vt_al = const.tile([P, G, 4], BF16)
        braw = const.tile([P, 2 * 4, SC], BF16)
        bcodes = const.tile([P, G, SC], U32, align_bytes=64)
        bscl = const.tile([P, G, SC], U8, align_bytes=64)
        thr = const.tile([P, 16], F32)

        def load_b(g):
            nc.sync.dma_start(out=braw[:, 4 * g : 4 * g + 4, :], in_=bv[g])

        def load_x(i):
            xt = xin.tile([P, JT, B], BF16, name="xt")
            nc.sync.dma_start(out=xt[:], in_=xv[i])
            x_t[i] = xt

        x0_t = {}

        def load_x0(g, b):
            js = slice(2 * b, 2 * b + 2) if g == 0 else slice(0, JT)
            xt = const.tile([P, js.stop - js.start, 512], BF16, name="x0_%d%d" % (g, b))
            nc.sync.dma_start(out=xt[:], in_=xv[0][:, js, 512 * g : 512 * g + 512])
            for j in range(js.start, js.stop):
                x0_t[(g, j)] = xt[:, j - js.start, :]

        def x_cols(i, g, j, t):
            if i == 0:
                return x0_t[(g, j)][:, t:512:4]
            return x_t[i][:, j, 512 * g + t : 512 * (g + 1) : 4]

        def load_c(i):
            ct = cin.tile([P, JT, SC], BF16, name="ct")
            nc.sync.dma_start(out=ct[:].rearrange("p j n -> p (j n)"), in_=cv[i])
            c_t[i] = ct

        for g in range(G):
            bg = const.tile([P, SC, 4], BF16, align_bytes=64, name="bgrp%d" % g)
            bgrp[g] = bg

        def regroup_b(g, half, eng):
            cols = slice(512 * half, 512 * half + 512)
            dst = bgrp[g][:, cols, :].rearrange("p (c i) t -> p c t i", i=4)
            src = braw[:, 4 * g : 4 * g + 4, cols].rearrange("p t (c i) -> p c t i", i=4)
            if eng == "s":
                nc.scalar.copy(out=dst, in_=src)
            else:
                nc.gpsimd.tensor_scalar(out=dst, in0=src, scalar1=1.0, scalar2=0.0, op0=ALU.mult, op1=ALU.add)

        def quant_b(g):
            nc.vector.quantize_mx(
                out=bcodes[:, g, :].bitcast(FP8X4),
                scales=bscl[:, g, :],
                in_=bgrp[g][:].rearrange("p n t -> p (n t)"),
            )

        def transposes(v, halves=(0, 1)):
            for a in halves:
                i, g, b = units[v][a]
                bank = xtp.tile([P, 4, 256], BF16, tag="xt", name="bank")
                for t in range(4):
                    for jj in range(2):
                        nc.tensor.transpose(
                            bank[:, t, 128 * jj : 128 * jj + 128], x_cols(i, g, 2 * b + jj, t), ident[:]
                        )
                banks[(v, a)] = bank

        def copies(v, halves=(0, 1)):
            if 0 in halves:
                xs = work.tile([P, 2, 4, 256], BF16, name="xs", bufs=3)
                xs_t[v] = xs
            for a in halves:
                nc.scalar.copy(out=xs_t[v][:, a, :, :], in_=banks[(v, a)][:])

        def clamp(dst, src, ch):
            nc.vector.tensor_scalar(
                out=dst,
                in0=src,
                scalar1=thr[:, 8 + ch : 9 + ch],
                scalar2=thr[:, ch : ch + 1],
                op0=ALU.max,
                op1=ALU.min,
            )

        def clamps(v):
            cl = work.tile([P, 2, 4, 256], BF16, name="cl")
            xs = xs_t[v]
            g0 = units[v][0][1]
            g1 = units[v][1][1]
            if g0 == g1 and v > 0:
                for t in range(4):
                    clamp(cl[:, :, t, :], xs[:, :, t, :], 4 * g0 + t)
            else:
                for a, ga in enumerate((g0, g1)):
                    for t in range(4):
                        clamp(cl[:, a, t, :], xs[:, a, t, :], 4 * ga + t)
            cl_t[v] = cl

        def damp(v):
            cl = cl_t[v]
            kp = work.tile([P, 2, 4, 256], BF16, name="kp")
            h = work.tile([P, 2, 256, 4], BF16, align_bytes=64, name="h")
            for a in range(2):
                nc.vector.tensor_tensor(out=kp[:, a, :, :], in0=cl[:, a, :, :], in1=banks[(v, a)][:], op=ALU.is_equal)
            for a in range(2):
                nc.vector.scalar_tensor_tensor(
                    out=h[:, a, :, :],
                    in0=kp[:, a, :, :].rearrange("p t s -> p s t"),
                    scalar=0.01,
                    in1=banks[(v, a)][:].rearrange("p t s -> p s t"),
                    op0=ALU.max,
                    op1=ALU.mult,
                )
            h_t[v] = h

        def quant(v):
            codes = work.tile([P, 2, 256], U32, align_bytes=64, name="codes", bufs=5)
            scl = work.tile([P, 2, 256], U8, align_bytes=64, name="scl", bufs=5)
            nc.vector.quantize_mx(
                out=codes[:].rearrange("p a s -> p (a s)").bitcast(FP8X4),
                scales=scl[:].rearrange("p a s -> p (a s)"),
                in_=h_t[v][:].rearrange("p a s t -> p (a s t)"),
            )
            for a, key in enumerate(units[v]):
                words[key] = (codes[:, a, :], scl[:, a, :])

        def add_cur_vector(i, acc, j, hf):
            cols = slice(512 * hf, 512 * hf + 512)
            nc.vector.tensor_tensor(out=o_t[i][:, j, cols], in0=acc[:], in1=c_t[i][:, j, cols], op=ALU.add)

        def job(i, b, vec_later=(), vec_now=False, tiles=(0, 1), wait=False):
            if b == 0 and 0 in tiles:
                ot = oout.tile([P, JT, SC], F32, name="ot")
                o_t[i] = ot
            later = []
            for n in range(2 * tiles[0], 2 * tiles[-1] + 2):
                jj, hf = divmod(n, 2)
                j = 2 * b + jj
                acc = accp.tile([P, 512], F32, name="acc")
                for g in range(G):
                    cw, sw = words[(i, g, b)]
                    nc.tensor.matmul_mx(
                        out=acc[:],
                        lhsT=cw[:, 128 * jj : 128 * jj + 128].bitcast(FP8X4),
                        lhsT_scale=sw[:, 128 * jj : 128 * jj + 128],
                        rhs=bcodes[:, g, 512 * hf : 512 * hf + 512].bitcast(FP8X4),
                        rhs_scale=bscl[:, g, 512 * hf : 512 * hf + 512],
                        start=(g == 0),
                        stop=(g == G - 1),
                    )
                cols = slice(512 * hf, 512 * hf + 512)
                if vec_now:
                    add_cur_vector(i, acc, j, hf)
                    if hf == 1:
                        nc.sync.dma_start(out=ov[i][:, SC * j : SC * j + SC], in_=o_t[i][:, j, :])
                elif n in vec_later:
                    later.append((i, acc, j, hf))
                else:
                    nc.scalar.copy(out=o_t[i][:, j, cols], in_=acc[:])
                    if hf == 0 and n + 1 not in vec_later:
                        continue
                    if hf == 1 and n - 1 not in vec_later:
                        cols = slice(0, SC)
                    if wait:
                        pend.append((i, j, cols))
                    else:
                        add_cur_gpsimd(i, j, cols)
            return later

        def add_cur_gpsimd(i, j, cols):
            nc.gpsimd.tensor_tensor(
                out=o_t[i][:, j, cols], in0=o_t[i][:, j, cols], in1=c_t[i][:, j, cols], op=ALU.add
            )

        def release(v):
            word = work.tile([P, 1], U32, name="word")
            nc.gpsimd.tensor_copy(out=word[:], in_=words[units[v][0]][0][:, 0:1])
            for i, j, cols in pend:
                add_cur_gpsimd(i, j, cols)
            pend.clear()

        def store(i, b):
            w = 2 * SC
            nc.sync.dma_start(
                out=ov[i][:, w * b : w * b + w], in_=o_t[i][:, 2 * b : 2 * b + 2, :].rearrange("p j n -> p (j n)")
            )

        load_x0(0, 0)
        nc.sync.dma_start(out=vt_av[:], in_=avail_bundle.rearrange("(g p t) -> p g t", p=P, t=4))
        nc.sync.dma_start(out=vt_al[:], in_=alloc_bundle.rearrange("(g p t) -> p g t", p=P, t=4))
        load_x0(0, 1)
        load_b(0)
        load_x0(1, 0)
        load_b(1)
        load_x(1)
        load_c(0)
        load_x(2)
        load_c(1)

        nc.vector.tensor_scalar(out=thr[:, 0:8], in0=vt_av[:].rearrange("p g t -> p (g t)"), scalar1=0.0, scalar2=None, op0=ALU.max)
        nc.vector.tensor_scalar(
            out=thr[:, 8:16], in0=vt_al[:].rearrange("p g t -> p (g t)"), scalar1=-1.0, scalar2=0.0, op0=ALU.mult, op1=ALU.min
        )
        transposes(0)
        copies(0)
        transposes(1)
        regroup_b(0, 0, "s")
        copies(1)
        regroup_b(0, 1, "s")
        regroup_b(1, 0, "s")
        regroup_b(1, 1, "g")

        first = {}
        second = {}
        done = {}
        for i in range(NST - 1):
            for b in range(2):
                first[2 * i + b + 2] = [(i, b, 0)]
                second[2 * i + b + 2] = [(i, b, 1)]
                done[2 * i + b + 2] = [(i, b)]
        second[NU - 2].append((NST - 2, 1, 0))
        first[NU - 1] = [(NST - 2, 1, 1), (NST - 1, 0, 0)]
        second[NU - 1] = [(NST - 1, 0, 1)]
        done[NU - 1].append((NST - 1, 0))

        held = []
        for v in range(NU):
            m = v // 2
            for i, b in done.get(v - 2, []):
                store(i, b)
            if v % 2 == 0:
                if m + 2 < NST:
                    load_c(m + 2)
                if m + 3 < NST:
                    load_x(m + 3)
            clamps(v)
            if v >= 1:
                quant(v - 1)
            if v in (1, 2):
                quant_b(v - 1)
            if pend:
                release(v - 1)
            later = []
            for i, b, tile in first.get(v, []):
                if i == NST - 1:
                    vec = ()
                elif v == NU - 1:
                    vec = (2, 3)
                else:
                    vec = (1,)
                later.extend(job(i, b, vec_later=vec, tiles=(tile,)))
            damp(v)
            if v + 2 < NU:
                transposes(v + 2, (0,))
                copies(v + 2, (0,))
            for i, b, tile in second.get(v, []):
                vec = (2, 3) if i == NST - 1 else ()
                held.extend(job(i, b, vec_later=vec, tiles=(tile,), wait=v < NU - 2))
            if v + 2 < NU:
                transposes(v + 2, (1,))
                copies(v + 2, (1,))
            for i, acc, j, hf in later:
                add_cur_vector(i, acc, j, hf)
        quant(NU - 1)
        for i, acc, j, hf in held:
            add_cur_vector(i, acc, j, hf)
        store(NST - 2, 0)
        store(NST - 2, 1)
        store(NST - 1, 0)
        job(NST - 1, 1, vec_now=True)
